import numpy as np
import ml_dtypes


def mxq(x, axis, fmt="e4m3"):
    dtype, down = {"e4m3": (ml_dtypes.float8_e4m3fn, 7), "e5m2": (ml_dtypes.float8_e5m2, 14)}[fmt]
    v = np.moveaxis(np.asarray(x, np.float32).astype(ml_dtypes.bfloat16).astype(np.float64), axis, -1)
    blocks = v.reshape(v.shape[:-1] + (-1, 32))
    amax = np.abs(blocks).max(-1, keepdims=True)
    byte = np.maximum(np.where(amax > 0, np.frexp(amax)[1] - 1 + 127, 0) - down, 1)
    scale = np.exp2(byte - 127.0)
    codes = (blocks / scale).astype(np.float32).astype(dtype).astype(np.float64)
    return np.moveaxis((codes * scale).reshape(v.shape), -1, axis)


WIDE = False


def mx_kscale(k):
    if not WIDE:
        return np.ones(k)
    levels = np.array([10, -10, 5, -5, 0])
    a = np.random.permutation(np.resize(levels, k // 512 * 4)).reshape(k // 512, 4)
    idx = np.arange(k)
    return np.exp2(a[idx // 512, idx % 128 // 32])


BF16 = ml_dtypes.bfloat16


def bf(x):
    return np.asarray(x, np.float32).astype(BF16)


def f64(x):
    return np.asarray(x).astype(np.float64)


E2M1 = np.array([0.0, 0.5, 1.0, 1.5, 2.0, 3.0, 4.0, 6.0, -0.0, -0.5, -1.0, -1.5, -2.0, -3.0, -4.0, -6.0])


def pack_weight(w, fmt):
    k, n = w.shape
    w = f64(bf(w)).reshape(k // 32, 32, n)
    amax = np.abs(w).max(1)
    if fmt == "e4m3":
        byte = np.frexp(amax)[1] - 1 + 127 - 7
    else:
        mant, ex = np.frexp(amax / 6.0)
        byte = np.where(mant > 0.5, ex, ex - 1) + 127
    byte = np.clip(np.where(amax > 0, byte, 1), 1, 254)
    scaled = (w * np.exp2(127.0 - byte)[:, None, :]).reshape(k, n).astype(np.float32)
    by_word = np.ascontiguousarray(scaled.reshape(k // 512, 128, 4, n).transpose(0, 1, 3, 2))
    if fmt == "e4m3":
        words = by_word.astype(ml_dtypes.float8_e4m3fn).view(np.uint8)
    else:
        c = by_word.astype(ml_dtypes.float4_e2m1fn).view(np.uint8) & 0xF
        words = c[..., 0::2] | (c[..., 1::2] << 4)
    return np.ascontiguousarray(words), np.ascontiguousarray(byte.astype(np.uint8).reshape(k // 512, 16, n))


def unpack_weight(words, scales, fmt):
    g, p, n, _ = words.shape
    if fmt == "e4m3":
        vals = np.ascontiguousarray(words).view(ml_dtypes.float8_e4m3fn).astype(np.float64)
    else:
        nib = np.empty((g, p, n, 4), np.uint8)
        nib[..., 0::2] = words & 0xF
        nib[..., 1::2] = words >> 4
        vals = E2M1[nib]
    vals = vals * np.repeat(np.exp2(scales.astype(np.float64) - 127.0), 8, axis=1)[..., None]
    return vals.transpose(0, 1, 3, 2).reshape(g * 512, n)


B, S, D, F = 2, 64, 2048, 4096


def silu(v):
    return v / (1.0 + np.exp(-v))


def setup_inputs():
    s, t = mx_kscale(D), mx_kscale(F)
    x = bf(np.random.standard_normal((B, S, D)) * s)
    gate_words, gate_scales = pack_weight((np.random.standard_normal((F, D)) * 1.0 / np.sqrt(D) / s[None, :]).T, "e4m3")
    up_words, up_scales = pack_weight((np.random.standard_normal((F, D)) * 1.0 / np.sqrt(D) / s[None, :] * t[:, None]).T, "e4m3")
    down_words, down_scales = pack_weight((np.random.standard_normal((D, F)) * 2.0 / np.sqrt(F) / t[None, :]).T, "e4m3")
    return {"x": x,
            "W_gate_words": gate_words, "W_gate_scales": gate_scales,
            "W_up_words": up_words, "W_up_scales": up_scales,
            "W_down_words": down_words, "W_down_scales": down_scales}


def reference(x, W_gate_words, W_gate_scales, W_up_words, W_up_scales, W_down_words, W_down_scales):
    out_shape = x.shape[:-1] + (W_down_words.shape[2],)
    xf = f64(x).reshape(-1, x.shape[-1])
    xq = mxq(xf, 1, "e4m3")
    up = xq @ unpack_weight(W_up_words, W_up_scales, "e4m3")
    gate = silu(xq @ unpack_weight(W_gate_words, W_gate_scales, "e4m3"))
    h = gate * up
    y = mxq(h, 1, "e4m3") @ unpack_weight(W_down_words, W_down_scales, "e4m3")
    return y.reshape(out_shape)

@@ -1,0 +1,177 @@
+from contextlib import ExitStack
+
+import concourse.mybir as mybir
+from concourse.masks import make_identity
+
+BF16 = mybir.dt.bfloat16
+F32 = mybir.dt.float32
+I32 = mybir.dt.int32
+U32 = mybir.dt.uint32
+U8 = mybir.dt.uint8
+FP8X4 = mybir.dt.float8_e4m3fn_x4
+
+P = 128
+PACK = 4
+K_PASS = P * PACK
+N_TILE = 512
+D_MODEL = 2048
+D_FF = 4096
+MODEL_GROUPS = D_MODEL // K_PASS
+FF_GROUPS = D_FF // K_PASS
+CHUNK = 1024
+CHUNK_GROUPS = CHUNK // K_PASS
+PLANES = 4
+QUADRANT = 32
+WEIGHT_BUFS = 10
+
+FLOPS = 2 * P * (2 * D_MODEL * D_FF + D_FF * D_MODEL)
+
+
+def load_scale_planes(nc, planes, scale_rows):
+    sets = planes.shape[1]
+    nc.vector.memset(planes.rearrange("p s n -> p (s n)").bitcast(I32), 0)
+    for s in range(sets):
+        for q in range(P // QUADRANT):
+            nc.sync.dma_start(
+                out=planes[QUADRANT * q : QUADRANT * q + 4 * PLANES, s, :].bitcast(I32),
+                in_=scale_rows[PLANES * s : PLANES * (s + 1), 4 * q : 4 * q + 4, :].bitcast(I32),
+            )
+
+
+def quantise_tokens(nc, flips, stage, identity, rows, codes, scales):
+    flipped = flips.tile([P, CHUNK_GROUPS, PACK, P], BF16)
+    for g in range(CHUNK_GROUPS):
+        for t in range(PACK):
+            nc.tensor.transpose(
+                flipped[:, g, t, :], rows[:, K_PASS * g + t : K_PASS * (g + 1) : PACK], identity
+            )
+    grouped = stage.tile([P, CHUNK_GROUPS, P, PACK], BF16, align_bytes=64)
+    nc.scalar.copy(out=grouped[:], in_=flipped[:].rearrange("p g t r -> p g r t"))
+    nc.vector.quantize_mx(
+        out=codes.bitcast(FP8X4),
+        scales=scales,
+        in_=grouped[:].rearrange("p g r t -> p (g r t)"),
+    )
+
+
+def tile_mixllamamlp_w_kernel(
+    tc, x, W_gate_words, W_gate_scales, W_up_words, W_up_scales, W_down_words, W_down_scales, out
+):
+    nc = tc.nc
+    x_rows = x.flatten_outer_dims()
+    out_rows = out.flatten_outer_dims()
+
+    with ExitStack() as ctx:
+        keep = ctx.enter_context(tc.tile_pool(name="keep", bufs=1))
+        weights = ctx.enter_context(tc.tile_pool(name="weights", bufs=WEIGHT_BUFS))
+        stage = ctx.enter_context(tc.tile_pool(name="stage", bufs=2))
+        results = ctx.enter_context(tc.tile_pool(name="results", bufs=4))
+        sums = ctx.enter_context(tc.psum_pool(name="sums", bufs=6))
+        flips = ctx.enter_context(tc.psum_pool(name="flips", bufs=2))
+
+        x_sb = keep.tile([P, D_MODEL], BF16)
+        nc.sync.dma_start(out=x_sb[:], in_=x_rows)
+
+        gate_planes = keep.tile([P, MODEL_GROUPS // PLANES, D_FF], U8, align_bytes=64)
+        up_planes = keep.tile([P, MODEL_GROUPS // PLANES, D_FF], U8, align_bytes=64)
+        down_planes = keep.tile([P, FF_GROUPS // PLANES, D_MODEL], U8, align_bytes=64)
+        load_scale_planes(nc, gate_planes[:], W_gate_scales)
+        load_scale_planes(nc, up_planes[:], W_up_scales)
+        load_scale_planes(nc, down_planes[:], W_down_scales)
+
+        gate_chunks = []
+        up_chunks = []
+        for c in range(D_FF // CHUNK):
+            chunk_bytes = slice(PACK * CHUNK * c, PACK * CHUNK * (c + 1))
+            for chunks, words in ((gate_chunks, W_gate_words), (up_chunks, W_up_words)):
+                w_chunk = weights.tile([P, MODEL_GROUPS, CHUNK], U32, tag="w", align_bytes=64)
+                nc.sync.dma_start(
+                    out=w_chunk[:].bitcast(I32),
+                    in_=words.rearrange("g p n t -> p g (n t)")[:, :, chunk_bytes].bitcast(I32),
+                )
+                chunks.append(w_chunk)
+
+        down_pairs = []
+        for pair in range(FF_GROUPS // 2):
+            w_pair = weights.tile([P, 2, D_MODEL], U32, tag="w", align_bytes=64)
+            for i in range(2):
+                nc.sync.dma_start(
+                    out=w_pair[:, i, :].bitcast(I32),
+                    in_=W_down_words[2 * pair + i].rearrange("p n t -> p (n t)").bitcast(I32),
+                )
+            down_pairs.append(w_pair)
+
+        identity = keep.tile([P, P], BF16)
+        make_identity(nc, identity[:])
+        x_codes = keep.tile([P, MODEL_GROUPS * P], U32, align_bytes=64)
+        x_scales = keep.tile([P, MODEL_GROUPS * P], U8, align_bytes=64)
+        h_codes = keep.tile([P, FF_GROUPS * P], U32, align_bytes=64)
+        h_scales = keep.tile([P, FF_GROUPS * P], U8, align_bytes=64)
+        for c in range(D_MODEL // CHUNK):
+            token_cols = slice(CHUNK_GROUPS * P * c, CHUNK_GROUPS * P * (c + 1))
+            quantise_tokens(
+                nc, flips, stage, identity[:], x_sb[:, CHUNK * c : CHUNK * (c + 1)],
+                x_codes[:, token_cols], x_scales[:, token_cols],
+            )
+
+        def stage1_sum(w_chunk, planes, c, j):
+            acc = sums.tile([P, N_TILE], F32, tag="sum")
+            first = CHUNK * c + N_TILE * j
+            for g in range(MODEL_GROUPS):
+                nc.tensor.matmul_mx(
+                    out=acc[:],
+                    lhsT=x_codes[:, P * g : P * (g + 1)].bitcast(FP8X4),
+                    lhsT_scale=x_scales[:, P * g : P * (g + 1)],
+                    rhs=w_chunk[:, g, N_TILE * j : N_TILE * (j + 1)].bitcast(FP8X4),
+                    rhs_scale=planes[4 * g : P, 0, first : first + N_TILE],
+                    start=(g == 0),
+                    stop=(g == MODEL_GROUPS - 1),
+                )
+            return acc
+
+        for c in range(D_FF // CHUNK):
+            gate_act = stage.tile([P, CHUNK], F32)
+            h_rows = stage.tile([P, CHUNK], BF16)
+            for j in range(CHUNK // N_TILE):
+                gate_sum = stage1_sum(gate_chunks[c], gate_planes, c, j)
+                nc.scalar.activation(
+                    out=gate_act[:, N_TILE * j : N_TILE * (j + 1)], in_=gate_sum[:],
+                    func=mybir.ActivationFunctionType.Silu,
+                )
+            for j in range(CHUNK // N_TILE):
+                cols = slice(N_TILE * j, N_TILE * (j + 1))
+                up_sum = stage1_sum(up_chunks[c], up_planes, c, j)
+                nc.vector.tensor_tensor(
+                    out=h_rows[:, cols], in0=gate_act[:, cols], in1=up_sum[:],
+                    op=mybir.AluOpType.mult,
+                )
+            token_cols = slice(CHUNK_GROUPS * P * c, CHUNK_GROUPS * P * (c + 1))
+            quantise_tokens(
+                nc, flips, stage, identity[:], h_rows[:],
+                h_codes[:, token_cols], h_scales[:, token_cols],
+            )
+
+        y_sums = []
+        for j in range(D_MODEL // N_TILE):
+            y_sum = sums.tile([P, N_TILE], F32, tag="sum")
+            y_sums.append(y_sum)
+        for g in range(FF_GROUPS):
+            for j in range(D_MODEL // N_TILE):
+                cols = slice(N_TILE * j, N_TILE * (j + 1))
+                nc.tensor.matmul_mx(
+                    out=y_sums[j][:],
+                    lhsT=h_codes[:, P * g : P * (g + 1)].bitcast(FP8X4),
+                    lhsT_scale=h_scales[:, P * g : P * (g + 1)],
+                    rhs=down_pairs[g // 2][:, g % 2, cols].bitcast(FP8X4),
+                    rhs_scale=down_planes[4 * (g % PLANES) : P, g // PLANES, cols],
+                    start=(g == 0),
+                    stop=(g == FF_GROUPS - 1),
+                )
+        for j in range(D_MODEL // N_TILE):
+            cols = slice(N_TILE * j, N_TILE * (j + 1))
+            y = results.tile([P, N_TILE], F32)
+            if j % 2 == 0:
+                nc.vector.tensor_copy(out=y[:], in_=y_sums[j][:])
+            else:
+                nc.scalar.copy(out=y[:], in_=y_sums[j][:])
+            nc.sync.dma_start(out=out_rows[:, cols], in_=y[:])

@@ -32,9 +32,9 @@ def load_scale_planes(nc, planes, scale_rows):
     nc.vector.memset(planes.rearrange("p s n -> p (s n)").bitcast(I32), 0)
     for s in range(sets):
         for q in range(P // QUADRANT):
-            nc.sync.dma_start(
-                out=planes[QUADRANT * q : QUADRANT * q + 4 * PLANES, s, :].bitcast(I32),
-                in_=scale_rows[PLANES * s : PLANES * (s + 1), 4 * q : 4 * q + 4, :].bitcast(I32),
+            nc.gpsimd.dma_start(
+                out=planes[QUADRANT * q : QUADRANT * q + 4 * PLANES, s, :].bitcast(F32),
+                in_=scale_rows[PLANES * s : PLANES * (s + 1), 4 * q : 4 * q + 4, :].bitcast(F32),
             )
 
 
@@ -69,6 +69,9 @@ def tile_mixllamamlp_w_kernel(
         sums = ctx.enter_context(tc.psum_pool(name="sums", bufs=6))
         flips = ctx.enter_context(tc.psum_pool(name="flips", bufs=2))
 
+        identity = keep.tile([P, P], BF16)
+        make_identity(nc, identity[:])
+
         x_sb = keep.tile([P, D_MODEL], BF16)
         nc.sync.dma_start(out=x_sb[:], in_=x_rows)
 
@@ -101,8 +104,6 @@ def tile_mixllamamlp_w_kernel(
                 )
             down_pairs.append(w_pair)
 
-        identity = keep.tile([P, P], BF16)
-        make_identity(nc, identity[:])
         x_codes = keep.tile([P, MODEL_GROUPS * P], U32, align_bytes=64)
         x_scales = keep.tile([P, MODEL_GROUPS * P], U8, align_bytes=64)
         h_codes = keep.tile([P, FF_GROUPS * P], U32, align_bytes=64)

@@ -14,14 +14,18 @@ P = 128
 PACK = 4
 K_PASS = P * PACK
 N_TILE = 512
+PSUM_BANKS = 8
 D_MODEL = 2048
 D_FF = 4096
 MODEL_GROUPS = D_MODEL // K_PASS
 FF_GROUPS = D_FF // K_PASS
-CHUNK = 1024
-CHUNK_GROUPS = CHUNK // K_PASS
+FF_TILES = D_FF // N_TILE
+MODEL_TILES = D_MODEL // N_TILE
+FLIP_GROUPS = 2
+FLIP_COLS = FLIP_GROUPS * K_PASS
 PLANES = 4
 QUADRANT = 32
+WEIGHT_WORDS = D_FF
 WEIGHT_BUFS = 10
 
 FLOPS = 2 * P * (2 * D_MODEL * D_FF + D_FF * D_MODEL)
@@ -32,20 +36,20 @@ def load_scale_planes(nc, planes, scale_rows):
     nc.vector.memset(planes.rearrange("p s n -> p (s n)").bitcast(I32), 0)
     for s in range(sets):
         for q in range(P // QUADRANT):
-            nc.gpsimd.dma_start(
-                out=planes[QUADRANT * q : QUADRANT * q + 4 * PLANES, s, :].bitcast(F32),
-                in_=scale_rows[PLANES * s : PLANES * (s + 1), 4 * q : 4 * q + 4, :].bitcast(F32),
+            nc.sync.dma_start(
+                out=planes[QUADRANT * q : QUADRANT * q + 4 * PLANES, s, :].bitcast(I32),
+                in_=scale_rows[PLANES * s : PLANES * (s + 1), 4 * q : 4 * q + 4, :].bitcast(I32),
             )
 
 
-def quantise_tokens(nc, flips, stage, identity, rows, codes, scales):
-    flipped = flips.tile([P, CHUNK_GROUPS, PACK, P], BF16)
-    for g in range(CHUNK_GROUPS):
+def quantise_tokens(nc, banks, stage, identity, rows, codes, scales):
+    flipped = banks.tile([P, FLIP_GROUPS, PACK, P], BF16, tag="bank")
+    for g in range(FLIP_GROUPS):
         for t in range(PACK):
             nc.tensor.transpose(
                 flipped[:, g, t, :], rows[:, K_PASS * g + t : K_PASS * (g + 1) : PACK], identity
             )
-    grouped = stage.tile([P, CHUNK_GROUPS, P, PACK], BF16, align_bytes=64)
+    grouped = stage.tile([P, FLIP_GROUPS, P, PACK], BF16, align_bytes=64)
     nc.scalar.copy(out=grouped[:], in_=flipped[:].rearrange("p g t r -> p g r t"))
     nc.vector.quantize_mx(
         out=codes.bitcast(FP8X4),
@@ -65,12 +69,8 @@ def tile_mixllamamlp_w_kernel(
         keep = ctx.enter_context(tc.tile_pool(name="keep", bufs=1))
         weights = ctx.enter_context(tc.tile_pool(name="weights", bufs=WEIGHT_BUFS))
         stage = ctx.enter_context(tc.tile_pool(name="stage", bufs=2))
-        results = ctx.enter_context(tc.tile_pool(name="results", bufs=4))
-        sums = ctx.enter_context(tc.psum_pool(name="sums", bufs=6))
-        flips = ctx.enter_context(tc.psum_pool(name="flips", bufs=2))
-
-        identity = keep.tile([P, P], BF16)
-        make_identity(nc, identity[:])
+        results = ctx.enter_context(tc.tile_pool(name="results", bufs=MODEL_TILES))
+        banks = ctx.enter_context(tc.psum_pool(name="banks", bufs=PSUM_BANKS))
 
         x_sb = keep.tile([P, D_MODEL], BF16)
         nc.sync.dma_start(out=x_sb[:], in_=x_rows)
@@ -82,97 +82,93 @@ def tile_mixllamamlp_w_kernel(
         load_scale_planes(nc, up_planes[:], W_up_scales)
         load_scale_planes(nc, down_planes[:], W_down_scales)
 
-        gate_chunks = []
-        up_chunks = []
-        for c in range(D_FF // CHUNK):
-            chunk_bytes = slice(PACK * CHUNK * c, PACK * CHUNK * (c + 1))
-            for chunks, words in ((gate_chunks, W_gate_words), (up_chunks, W_up_words)):
-                w_chunk = weights.tile([P, MODEL_GROUPS, CHUNK], U32, tag="w", align_bytes=64)
+        gate_groups = []
+        up_groups = []
+        for groups, words in ((gate_groups, W_gate_words), (up_groups, W_up_words)):
+            for g in range(MODEL_GROUPS):
+                w_group = weights.tile([P, WEIGHT_WORDS], U32, tag="w", align_bytes=64)
                 nc.sync.dma_start(
-                    out=w_chunk[:].bitcast(I32),
-                    in_=words.rearrange("g p n t -> p g (n t)")[:, :, chunk_bytes].bitcast(I32),
+                    out=w_group[:].bitcast(I32),
+                    in_=words[g].rearrange("p n t -> p (n t)").bitcast(I32),
                 )
-                chunks.append(w_chunk)
+                groups.append(w_group)
 
-        down_pairs = []
+        down_groups = []
         for pair in range(FF_GROUPS // 2):
             w_pair = weights.tile([P, 2, D_MODEL], U32, tag="w", align_bytes=64)
-            for i in range(2):
-                nc.sync.dma_start(
-                    out=w_pair[:, i, :].bitcast(I32),
-                    in_=W_down_words[2 * pair + i].rearrange("p n t -> p (n t)").bitcast(I32),
-                )
-            down_pairs.append(w_pair)
+            down_groups.append(w_pair[:, 0, :])
+            down_groups.append(w_pair[:, 1, :])
+        for g in range(FF_GROUPS - 1):
+            nc.sync.dma_start(
+                out=down_groups[g].bitcast(I32),
+                in_=W_down_words[g].rearrange("p n t -> p (n t)").bitcast(I32),
+            )
+        last_words = W_down_words[FF_GROUPS - 1].rearrange("p n t -> p (n t)").bitcast(I32)
+        for j in range(MODEL_TILES):
+            cols = slice(N_TILE * j, N_TILE * (j + 1))
+            nc.sync.dma_start(
+                out=down_groups[FF_GROUPS - 1][:, cols].bitcast(I32), in_=last_words[:, cols]
+            )
 
+        identity = keep.tile([P, P], BF16)
+        make_identity(nc, identity[:])
         x_codes = keep.tile([P, MODEL_GROUPS * P], U32, align_bytes=64)
         x_scales = keep.tile([P, MODEL_GROUPS * P], U8, align_bytes=64)
-        h_codes = keep.tile([P, FF_GROUPS * P], U32, align_bytes=64)
-        h_scales = keep.tile([P, FF_GROUPS * P], U8, align_bytes=64)
-        for c in range(D_MODEL // CHUNK):
-            token_cols = slice(CHUNK_GROUPS * P * c, CHUNK_GROUPS * P * (c + 1))
+        for c in range(D_MODEL // FLIP_COLS):
+            token_cols = slice(FLIP_GROUPS * P * c, FLIP_GROUPS * P * (c + 1))
             quantise_tokens(
-                nc, flips, stage, identity[:], x_sb[:, CHUNK * c : CHUNK * (c + 1)],
+                nc, banks, stage, identity[:], x_sb[:, FLIP_COLS * c : FLIP_COLS * (c + 1)],
                 x_codes[:, token_cols], x_scales[:, token_cols],
             )
 
-        def stage1_sum(w_chunk, planes, c, j):
-            acc = sums.tile([P, N_TILE], F32, tag="sum")
-            first = CHUNK * c + N_TILE * j
-            for g in range(MODEL_GROUPS):
-                nc.tensor.matmul_mx(
-                    out=acc[:],
-                    lhsT=x_codes[:, P * g : P * (g + 1)].bitcast(FP8X4),
-                    lhsT_scale=x_scales[:, P * g : P * (g + 1)],
-                    rhs=w_chunk[:, g, N_TILE * j : N_TILE * (j + 1)].bitcast(FP8X4),
-                    rhs_scale=planes[4 * g : P, 0, first : first + N_TILE],
-                    start=(g == 0),
-                    stop=(g == MODEL_GROUPS - 1),
-                )
-            return acc
+        def weight_passes(n_tiles, tokens, token_scales, groups, planes):
+            sums = []
+            for j in range(n_tiles):
+                acc = banks.tile([P, N_TILE], F32, tag="bank")
+                sums.append(acc)
+            for g in range(len(groups)):
+                for j in range(n_tiles):
+                    cols = slice(N_TILE * j, N_TILE * (j + 1))
+                    nc.tensor.matmul_mx(
+                        out=sums[j][:],
+                        lhsT=tokens[:, P * g : P * (g + 1)].bitcast(FP8X4),
+                        lhsT_scale=token_scales[:, P * g : P * (g + 1)],
+                        rhs=groups[g][:, cols].bitcast(FP8X4),
+                        rhs_scale=planes[4 * (g % PLANES) : P, g // PLANES, cols],
+                        start=(g == 0),
+                        stop=(g == len(groups) - 1),
+                    )
+            return sums
 
-        for c in range(D_FF // CHUNK):
-            gate_act = stage.tile([P, CHUNK], F32)
-            h_rows = stage.tile([P, CHUNK], BF16)
-            for j in range(CHUNK // N_TILE):
-                gate_sum = stage1_sum(gate_chunks[c], gate_planes, c, j)
-                nc.scalar.activation(
-                    out=gate_act[:, N_TILE * j : N_TILE * (j + 1)], in_=gate_sum[:],
-                    func=mybir.ActivationFunctionType.Silu,
-                )
-            for j in range(CHUNK // N_TILE):
-                cols = slice(N_TILE * j, N_TILE * (j + 1))
-                up_sum = stage1_sum(up_chunks[c], up_planes, c, j)
-                nc.vector.tensor_tensor(
-                    out=h_rows[:, cols], in0=gate_act[:, cols], in1=up_sum[:],
-                    op=mybir.AluOpType.mult,
-                )
-            token_cols = slice(CHUNK_GROUPS * P * c, CHUNK_GROUPS * P * (c + 1))
+        gate_act = keep.tile([P, D_FF], F32)
+        gate_sums = weight_passes(FF_TILES, x_codes, x_scales, gate_groups, gate_planes)
+        for j in range(FF_TILES):
+            nc.scalar.activation(
+                out=gate_act[:, N_TILE * j : N_TILE * (j + 1)], in_=gate_sums[j][:],
+                func=mybir.ActivationFunctionType.Silu,
+            )
+        h_rows = keep.tile([P, D_FF], BF16)
+        h_codes = keep.tile([P, FF_GROUPS * P], U32, align_bytes=64)
+        h_scales = keep.tile([P, FF_GROUPS * P], U8, align_bytes=64)
+        up_sums = weight_passes(FF_TILES, x_codes, x_scales, up_groups, up_planes)
+        for j in range(FF_TILES):
+            cols = slice(N_TILE * j, N_TILE * (j + 1))
+            nc.vector.tensor_tensor(
+                out=h_rows[:, cols], in0=gate_act[:, cols], in1=up_sums[j][:],
+                op=mybir.AluOpType.mult,
+            )
+        for c in range(D_FF // FLIP_COLS):
+            token_cols = slice(FLIP_GROUPS * P * c, FLIP_GROUPS * P * (c + 1))
             quantise_tokens(
-                nc, flips, stage, identity[:], h_rows[:],
+                nc, banks, stage, identity[:], h_rows[:, FLIP_COLS * c : FLIP_COLS * (c + 1)],
                 h_codes[:, token_cols], h_scales[:, token_cols],
             )
 
-        y_sums = []
-        for j in range(D_MODEL // N_TILE):
-            y_sum = sums.tile([P, N_TILE], F32, tag="sum")
-            y_sums.append(y_sum)
-        for g in range(FF_GROUPS):
-            for j in range(D_MODEL // N_TILE):
-                cols = slice(N_TILE * j, N_TILE * (j + 1))
-                nc.tensor.matmul_mx(
-                    out=y_sums[j][:],
-                    lhsT=h_codes[:, P * g : P * (g + 1)].bitcast(FP8X4),
-                    lhsT_scale=h_scales[:, P * g : P * (g + 1)],
-                    rhs=down_pairs[g // 2][:, g % 2, cols].bitcast(FP8X4),
-                    rhs_scale=down_planes[4 * (g % PLANES) : P, g // PLANES, cols],
-                    start=(g == 0),
-                    stop=(g == FF_GROUPS - 1),
-                )
-        for j in range(D_MODEL // N_TILE):
-            cols = slice(N_TILE * j, N_TILE * (j + 1))
+        y_sums = weight_passes(MODEL_TILES, h_codes, h_scales, down_groups, down_planes)
+        for j in range(MODEL_TILES):
             y = results.tile([P, N_TILE], F32)
             if j % 2 == 0:
                 nc.vector.tensor_copy(out=y[:], in_=y_sums[j][:])
             else:
                 nc.scalar.copy(out=y[:], in_=y_sums[j][:])
-            nc.sync.dma_start(out=out_rows[:, cols], in_=y[:])
+            nc.sync.dma_start(out=out_rows[:, N_TILE * j : N_TILE * (j + 1)], in_=y[:])

@@ -36,10 +36,12 @@ def load_scale_planes(nc, planes, scale_rows):
     nc.vector.memset(planes.rearrange("p s n -> p (s n)").bitcast(I32), 0)
     for s in range(sets):
         for q in range(P // QUADRANT):
-            nc.sync.dma_start(
-                out=planes[QUADRANT * q : QUADRANT * q + 4 * PLANES, s, :].bitcast(I32),
-                in_=scale_rows[PLANES * s : PLANES * (s + 1), 4 * q : 4 * q + 4, :].bitcast(I32),
-            )
+            sbuf_rows = planes[QUADRANT * q : QUADRANT * q + 4 * PLANES, s, :]
+            hbm_rows = scale_rows[PLANES * s : PLANES * (s + 1), 4 * q : 4 * q + 4, :]
+            if QUADRANT * q < P // 2:
+                nc.sync.dma_start(out=sbuf_rows.bitcast(I32), in_=hbm_rows.bitcast(I32))
+            else:
+                nc.gpsimd.dma_start(out=sbuf_rows.bitcast(F32), in_=hbm_rows.bitcast(F32))
 
 
 def quantise_tokens(nc, banks, stage, identity, rows, codes, scales):
@@ -71,6 +73,9 @@ def tile_mixllamamlp_w_kernel(
         stage = ctx.enter_context(tc.tile_pool(name="stage", bufs=2))
         results = ctx.enter_context(tc.tile_pool(name="results", bufs=MODEL_TILES))
         banks = ctx.enter_context(tc.psum_pool(name="banks", bufs=PSUM_BANKS))
+
+        identity = keep.tile([P, P], BF16)
+        make_identity(nc, identity[:])
 
         x_sb = keep.tile([P, D_MODEL], BF16)
         nc.sync.dma_start(out=x_sb[:], in_=x_rows)
@@ -110,8 +115,6 @@ def tile_mixllamamlp_w_kernel(
                 out=down_groups[FF_GROUPS - 1][:, cols].bitcast(I32), in_=last_words[:, cols]
             )
 
-        identity = keep.tile([P, P], BF16)
-        make_identity(nc, identity[:])
         x_codes = keep.tile([P, MODEL_GROUPS * P], U32, align_bytes=64)
         x_scales = keep.tile([P, MODEL_GROUPS * P], U8, align_bytes=64)
         for c in range(D_MODEL // FLIP_COLS):

@@ -77,43 +77,47 @@ def tile_mixllamamlp_w_kernel(
         identity = keep.tile([P, P], BF16)
         make_identity(nc, identity[:])
 
-        x_sb = keep.tile([P, D_MODEL], BF16)
-        nc.sync.dma_start(out=x_sb[:], in_=x_rows)
+        with tc.manual_schedule(engines={mybir.EngineType.SP}):
+            x_sb = keep.tile([P, D_MODEL], BF16)
+            nc.sync.dma_start(out=x_sb[:], in_=x_rows)
 
-        gate_planes = keep.tile([P, MODEL_GROUPS // PLANES, D_FF], U8, align_bytes=64)
-        up_planes = keep.tile([P, MODEL_GROUPS // PLANES, D_FF], U8, align_bytes=64)
-        down_planes = keep.tile([P, FF_GROUPS // PLANES, D_MODEL], U8, align_bytes=64)
-        load_scale_planes(nc, gate_planes[:], W_gate_scales)
-        load_scale_planes(nc, up_planes[:], W_up_scales)
-        load_scale_planes(nc, down_planes[:], W_down_scales)
-
-        gate_groups = []
-        up_groups = []
-        for groups, words in ((gate_groups, W_gate_words), (up_groups, W_up_words)):
-            for g in range(MODEL_GROUPS):
+            gate_planes = keep.tile([P, MODEL_GROUPS // PLANES, D_FF], U8, align_bytes=64)
+            up_planes = keep.tile([P, MODEL_GROUPS // PLANES, D_FF], U8, align_bytes=64)
+            down_planes = keep.tile([P, FF_GROUPS // PLANES, D_MODEL], U8, align_bytes=64)
+            def load_group(words, g):
                 w_group = weights.tile([P, WEIGHT_WORDS], U32, tag="w", align_bytes=64)
                 nc.sync.dma_start(
                     out=w_group[:].bitcast(I32),
                     in_=words[g].rearrange("p n t -> p (n t)").bitcast(I32),
                 )
-                groups.append(w_group)
+                return w_group
 
-        down_groups = []
-        for pair in range(FF_GROUPS // 2):
-            w_pair = weights.tile([P, 2, D_MODEL], U32, tag="w", align_bytes=64)
-            down_groups.append(w_pair[:, 0, :])
-            down_groups.append(w_pair[:, 1, :])
-        for g in range(FF_GROUPS - 1):
-            nc.sync.dma_start(
-                out=down_groups[g].bitcast(I32),
-                in_=W_down_words[g].rearrange("p n t -> p (n t)").bitcast(I32),
-            )
-        last_words = W_down_words[FF_GROUPS - 1].rearrange("p n t -> p (n t)").bitcast(I32)
-        for j in range(MODEL_TILES):
-            cols = slice(N_TILE * j, N_TILE * (j + 1))
-            nc.sync.dma_start(
-                out=down_groups[FF_GROUPS - 1][:, cols].bitcast(I32), in_=last_words[:, cols]
-            )
+            load_scale_planes(nc, gate_planes[:], W_gate_scales)
+            gate_groups = [load_group(W_gate_words, 0)]
+            load_scale_planes(nc, up_planes[:], W_up_scales)
+            load_scale_planes(nc, down_planes[:], W_down_scales)
+            for g in range(1, MODEL_GROUPS):
+                gate_groups.append(load_group(W_gate_words, g))
+            up_groups = []
+            for g in range(MODEL_GROUPS):
+                up_groups.append(load_group(W_up_words, g))
+
+            down_groups = []
+            for pair in range(FF_GROUPS // 2):
+                w_pair = weights.tile([P, 2, D_MODEL], U32, tag="w", align_bytes=64)
+                down_groups.append(w_pair[:, 0, :])
+                down_groups.append(w_pair[:, 1, :])
+            for g in range(FF_GROUPS - 1):
+                nc.sync.dma_start(
+                    out=down_groups[g].bitcast(I32),
+                    in_=W_down_words[g].rearrange("p n t -> p (n t)").bitcast(I32),
+                )
+            last_words = W_down_words[FF_GROUPS - 1].rearrange("p n t -> p (n t)").bitcast(I32)
+            for j in range(MODEL_TILES):
+                cols = slice(N_TILE * j, N_TILE * (j + 1))
+                nc.sync.dma_start(
+                    out=down_groups[FF_GROUPS - 1][:, cols].bitcast(I32), in_=last_words[:, cols]
+                )
 
         x_codes = keep.tile([P, MODEL_GROUPS * P], U32, align_bytes=64)
         x_scales = keep.tile([P, MODEL_GROUPS * P], U8, align_bytes=64)

@@ -21,11 +21,14 @@ MODEL_GROUPS = D_MODEL // K_PASS
 FF_GROUPS = D_FF // K_PASS
 FF_TILES = D_FF // N_TILE
 MODEL_TILES = D_MODEL // N_TILE
+Y_WIDTHS = (512, 512, 512, 256, 256)
+LAST_PIECES = ((0, 1024), (1024, 1536), (1536, 2048))
 FLIP_GROUPS = 2
 FLIP_COLS = FLIP_GROUPS * K_PASS
 PLANES = 4
 QUADRANT = 32
 WEIGHT_WORDS = D_FF
+WEIGHT_ALIGN = 256
 WEIGHT_BUFS = 10
 
 FLOPS = 2 * P * (2 * D_MODEL * D_FF + D_FF * D_MODEL)
@@ -85,7 +88,7 @@ def tile_mixllamamlp_w_kernel(
             up_planes = keep.tile([P, MODEL_GROUPS // PLANES, D_FF], U8, align_bytes=64)
             down_planes = keep.tile([P, FF_GROUPS // PLANES, D_MODEL], U8, align_bytes=64)
             def load_group(words, g):
-                w_group = weights.tile([P, WEIGHT_WORDS], U32, tag="w", align_bytes=64)
+                w_group = weights.tile([P, WEIGHT_WORDS], U32, tag="w", align_bytes=WEIGHT_ALIGN)
                 nc.sync.dma_start(
                     out=w_group[:].bitcast(I32),
                     in_=words[g].rearrange("p n t -> p (n t)").bitcast(I32),
@@ -104,7 +107,7 @@ def tile_mixllamamlp_w_kernel(
 
             down_groups = []
             for pair in range(FF_GROUPS // 2):
-                w_pair = weights.tile([P, 2, D_MODEL], U32, tag="w", align_bytes=64)
+                w_pair = weights.tile([P, 2, D_MODEL], U32, tag="w", align_bytes=WEIGHT_ALIGN)
                 down_groups.append(w_pair[:, 0, :])
                 down_groups.append(w_pair[:, 1, :])
             for g in range(FF_GROUPS - 1):
@@ -113,8 +116,8 @@ def tile_mixllamamlp_w_kernel(
                     in_=W_down_words[g].rearrange("p n t -> p (n t)").bitcast(I32),
                 )
             last_words = W_down_words[FF_GROUPS - 1].rearrange("p n t -> p (n t)").bitcast(I32)
-            for j in range(MODEL_TILES):
-                cols = slice(N_TILE * j, N_TILE * (j + 1))
+            for first, stop in LAST_PIECES:
+                cols = slice(first, stop)
                 nc.sync.dma_start(
                     out=down_groups[FF_GROUPS - 1][:, cols].bitcast(I32), in_=last_words[:, cols]
                 )
@@ -128,14 +131,16 @@ def tile_mixllamamlp_w_kernel(
                 x_codes[:, token_cols], x_scales[:, token_cols],
             )
 
-        def weight_passes(n_tiles, tokens, token_scales, groups, planes):
+        def weight_passes(widths, tokens, token_scales, groups, planes):
+            starts = []
             sums = []
-            for j in range(n_tiles):
-                acc = banks.tile([P, N_TILE], F32, tag="bank")
+            for j in range(len(widths)):
+                starts.append(sum(widths[:j]))
+                acc = banks.tile([P, widths[j]], F32, tag="bank")
                 sums.append(acc)
             for g in range(len(groups)):
-                for j in range(n_tiles):
-                    cols = slice(N_TILE * j, N_TILE * (j + 1))
+                for j in range(len(widths)):
+                    cols = slice(starts[j], starts[j] + widths[j])
                     nc.tensor.matmul_mx(
                         out=sums[j][:],
                         lhsT=tokens[:, P * g : P * (g + 1)].bitcast(FP8X4),
@@ -148,7 +153,7 @@ def tile_mixllamamlp_w_kernel(
             return sums
 
         gate_act = keep.tile([P, D_FF], F32)
-        gate_sums = weight_passes(FF_TILES, x_codes, x_scales, gate_groups, gate_planes)
+        gate_sums = weight_passes((N_TILE,) * FF_TILES, x_codes, x_scales, gate_groups, gate_planes)
         for j in range(FF_TILES):
             nc.scalar.activation(
                 out=gate_act[:, N_TILE * j : N_TILE * (j + 1)], in_=gate_sums[j][:],
@@ -157,7 +162,7 @@ def tile_mixllamamlp_w_kernel(
         h_rows = keep.tile([P, D_FF], BF16)
         h_codes = keep.tile([P, FF_GROUPS * P], U32, align_bytes=64)
         h_scales = keep.tile([P, FF_GROUPS * P], U8, align_bytes=64)
-        up_sums = weight_passes(FF_TILES, x_codes, x_scales, up_groups, up_planes)
+        up_sums = weight_passes((N_TILE,) * FF_TILES, x_codes, x_scales, up_groups, up_planes)
         for j in range(FF_TILES):
             cols = slice(N_TILE * j, N_TILE * (j + 1))
             nc.vector.tensor_tensor(
@@ -171,11 +176,15 @@ def tile_mixllamamlp_w_kernel(
                 h_codes[:, token_cols], h_scales[:, token_cols],
             )
 
-        y_sums = weight_passes(MODEL_TILES, h_codes, h_scales, down_groups, down_planes)
+        y_sums = weight_passes(Y_WIDTHS, h_codes, h_scales, down_groups, down_planes)
         for j in range(MODEL_TILES):
             y = results.tile([P, N_TILE], F32)
-            if j % 2 == 0:
-                nc.vector.tensor_copy(out=y[:], in_=y_sums[j][:])
+            if j < MODEL_TILES - 1:
+                if j % 2 == 0:
+                    nc.vector.tensor_copy(out=y[:], in_=y_sums[j][:])
+                else:
+                    nc.scalar.copy(out=y[:], in_=y_sums[j][:])
             else:
-                nc.scalar.copy(out=y[:], in_=y_sums[j][:])
+                nc.vector.tensor_copy(out=y[:, : N_TILE // 2], in_=y_sums[j][:])
+                nc.scalar.copy(out=y[:, N_TILE // 2 :], in_=y_sums[j + 1][:])
             nc.sync.dma_start(out=out_rows[:, N_TILE * j : N_TILE * (j + 1)], in_=y[:])

@@ -28,7 +28,8 @@ FLIP_COLS = FLIP_GROUPS * K_PASS
 PLANES = 4
 QUADRANT = 32
 WEIGHT_WORDS = D_FF
-WEIGHT_ALIGN = 256
+WEIGHT_ALIGN = 4096
+DMA_ALIGN = 256
 WEIGHT_BUFS = 10
 
 FLOPS = 2 * P * (2 * D_MODEL * D_FF + D_FF * D_MODEL)
@@ -81,12 +82,12 @@ def tile_mixllamamlp_w_kernel(
         make_identity(nc, identity[:])
 
         with tc.manual_schedule(engines={mybir.EngineType.SP}):
-            x_sb = keep.tile([P, D_MODEL], BF16)
+            x_sb = keep.tile([P, D_MODEL], BF16, align_bytes=DMA_ALIGN)
             nc.sync.dma_start(out=x_sb[:], in_=x_rows)
 
-            gate_planes = keep.tile([P, MODEL_GROUPS // PLANES, D_FF], U8, align_bytes=64)
-            up_planes = keep.tile([P, MODEL_GROUPS // PLANES, D_FF], U8, align_bytes=64)
-            down_planes = keep.tile([P, FF_GROUPS // PLANES, D_MODEL], U8, align_bytes=64)
+            gate_planes = keep.tile([P, MODEL_GROUPS // PLANES, D_FF], U8, align_bytes=DMA_ALIGN)
+            up_planes = keep.tile([P, MODEL_GROUPS // PLANES, D_FF], U8, align_bytes=DMA_ALIGN)
+            down_planes = keep.tile([P, FF_GROUPS // PLANES, D_MODEL], U8, align_bytes=DMA_ALIGN)
             def load_group(words, g):
                 w_group = weights.tile([P, WEIGHT_WORDS], U32, tag="w", align_bytes=WEIGHT_ALIGN)
                 nc.sync.dma_start(
@@ -178,7 +179,7 @@ def tile_mixllamamlp_w_kernel(
 
         y_sums = weight_passes(Y_WIDTHS, h_codes, h_scales, down_groups, down_planes)
         for j in range(MODEL_TILES):
-            y = results.tile([P, N_TILE], F32)
+            y = results.tile([P, N_TILE], F32, align_bytes=DMA_ALIGN)
             if j < MODEL_TILES - 1:
                 if j % 2 == 0:
                     nc.vector.tensor_copy(out=y[:], in_=y_sums[j][:])

from contextlib import ExitStack

import concourse.mybir as mybir
from concourse.masks import make_identity

BF16 = mybir.dt.bfloat16
F32 = mybir.dt.float32
I32 = mybir.dt.int32
U32 = mybir.dt.uint32
U8 = mybir.dt.uint8
FP8X4 = mybir.dt.float8_e4m3fn_x4

P = 128
PACK = 4
K_PASS = P * PACK
N_TILE = 512
PSUM_BANKS = 8
D_MODEL = 2048
D_FF = 4096
MODEL_GROUPS = D_MODEL // K_PASS
FF_GROUPS = D_FF // K_PASS
FF_TILES = D_FF // N_TILE
MODEL_TILES = D_MODEL // N_TILE
Y_WIDTHS = (512, 512, 512, 256, 256)
LAST_PIECES = ((0, 1024), (1024, 1536), (1536, 2048))
FLIP_GROUPS = 2
FLIP_COLS = FLIP_GROUPS * K_PASS
PLANES = 4
QUADRANT = 32
WEIGHT_WORDS = D_FF
WEIGHT_ALIGN = 4096
DMA_ALIGN = 256
WEIGHT_BUFS = 10

FLOPS = 2 * P * (2 * D_MODEL * D_FF + D_FF * D_MODEL)


def load_scale_planes(nc, planes, scale_rows):
    sets = planes.shape[1]
    nc.vector.memset(planes.rearrange("p s n -> p (s n)").bitcast(I32), 0)
    for s in range(sets):
        for q in range(P // QUADRANT):
            sbuf_rows = planes[QUADRANT * q : QUADRANT * q + 4 * PLANES, s, :]
            hbm_rows = scale_rows[PLANES * s : PLANES * (s + 1), 4 * q : 4 * q + 4, :]
            if QUADRANT * q < P // 2:
                nc.sync.dma_start(out=sbuf_rows.bitcast(I32), in_=hbm_rows.bitcast(I32))
            else:
                nc.gpsimd.dma_start(out=sbuf_rows.bitcast(F32), in_=hbm_rows.bitcast(F32))


def quantise_tokens(nc, banks, stage, identity, rows, codes, scales):
    flipped = banks.tile([P, FLIP_GROUPS, PACK, P], BF16, tag="bank")
    for g in range(FLIP_GROUPS):
        for t in range(PACK):
            nc.tensor.transpose(
                flipped[:, g, t, :], rows[:, K_PASS * g + t : K_PASS * (g + 1) : PACK], identity
            )
    grouped = stage.tile([P, FLIP_GROUPS, P, PACK], BF16, align_bytes=64)
    nc.scalar.copy(out=grouped[:], in_=flipped[:].rearrange("p g t r -> p g r t"))
    nc.vector.quantize_mx(
        out=codes.bitcast(FP8X4),
        scales=scales,
        in_=grouped[:].rearrange("p g r t -> p (g r t)"),
    )


def tile_mixllamamlp_w_kernel(
    tc, x, W_gate_words, W_gate_scales, W_up_words, W_up_scales, W_down_words, W_down_scales, out
):
    nc = tc.nc
    x_rows = x.flatten_outer_dims()
    out_rows = out.flatten_outer_dims()

    with ExitStack() as ctx:
        keep = ctx.enter_context(tc.tile_pool(name="keep", bufs=1))
        weights = ctx.enter_context(tc.tile_pool(name="weights", bufs=WEIGHT_BUFS))
        stage = ctx.enter_context(tc.tile_pool(name="stage", bufs=2))
        results = ctx.enter_context(tc.tile_pool(name="results", bufs=MODEL_TILES))
        banks = ctx.enter_context(tc.psum_pool(name="banks", bufs=PSUM_BANKS))

        identity = keep.tile([P, P], BF16)
        make_identity(nc, identity[:])

        with tc.manual_schedule(engines={mybir.EngineType.SP}):
            x_sb = keep.tile([P, D_MODEL], BF16, align_bytes=DMA_ALIGN)
            nc.sync.dma_start(out=x_sb[:], in_=x_rows)

            gate_planes = keep.tile([P, MODEL_GROUPS // PLANES, D_FF], U8, align_bytes=DMA_ALIGN)
            up_planes = keep.tile([P, MODEL_GROUPS // PLANES, D_FF], U8, align_bytes=DMA_ALIGN)
            down_planes = keep.tile([P, FF_GROUPS // PLANES, D_MODEL], U8, align_bytes=DMA_ALIGN)
            def load_group(words, g):
                w_group = weights.tile([P, WEIGHT_WORDS], U32, tag="w", align_bytes=WEIGHT_ALIGN)
                nc.sync.dma_start(
                    out=w_group[:].bitcast(I32),
                    in_=words[g].rearrange("p n t -> p (n t)").bitcast(I32),
                )
                return w_group

            load_scale_planes(nc, gate_planes[:], W_gate_scales)
            gate_groups = [load_group(W_gate_words, 0)]
            load_scale_planes(nc, up_planes[:], W_up_scales)
            load_scale_planes(nc, down_planes[:], W_down_scales)
            for g in range(1, MODEL_GROUPS):
                gate_groups.append(load_group(W_gate_words, g))
            up_groups = []
            for g in range(MODEL_GROUPS):
                up_groups.append(load_group(W_up_words, g))

            down_groups = []
            for pair in range(FF_GROUPS // 2):
                w_pair = weights.tile([P, 2, D_MODEL], U32, tag="w", align_bytes=WEIGHT_ALIGN)
                down_groups.append(w_pair[:, 0, :])
                down_groups.append(w_pair[:, 1, :])
            for g in range(FF_GROUPS - 1):
                nc.sync.dma_start(
                    out=down_groups[g].bitcast(I32),
                    in_=W_down_words[g].rearrange("p n t -> p (n t)").bitcast(I32),
                )
            last_words = W_down_words[FF_GROUPS - 1].rearrange("p n t -> p (n t)").bitcast(I32)
            for first, stop in LAST_PIECES:
                cols = slice(first, stop)
                nc.sync.dma_start(
                    out=down_groups[FF_GROUPS - 1][:, cols].bitcast(I32), in_=last_words[:, cols]
                )

        x_codes = keep.tile([P, MODEL_GROUPS * P], U32, align_bytes=64)
        x_scales = keep.tile([P, MODEL_GROUPS * P], U8, align_bytes=64)
        for c in range(D_MODEL // FLIP_COLS):
            token_cols = slice(FLIP_GROUPS * P * c, FLIP_GROUPS * P * (c + 1))
            quantise_tokens(
                nc, banks, stage, identity[:], x_sb[:, FLIP_COLS * c : FLIP_COLS * (c + 1)],
                x_codes[:, token_cols], x_scales[:, token_cols],
            )

        def weight_passes(widths, tokens, token_scales, groups, planes):
            starts = []
            sums = []
            for j in range(len(widths)):
                starts.append(sum(widths[:j]))
                acc = banks.tile([P, widths[j]], F32, tag="bank")
                sums.append(acc)
            for g in range(len(groups)):
                for j in range(len(widths)):
                    cols = slice(starts[j], starts[j] + widths[j])
                    nc.tensor.matmul_mx(
                        out=sums[j][:],
                        lhsT=tokens[:, P * g : P * (g + 1)].bitcast(FP8X4),
                        lhsT_scale=token_scales[:, P * g : P * (g + 1)],
                        rhs=groups[g][:, cols].bitcast(FP8X4),
                        rhs_scale=planes[4 * (g % PLANES) : P, g // PLANES, cols],
                        start=(g == 0),
                        stop=(g == len(groups) - 1),
                    )
            return sums

        gate_act = keep.tile([P, D_FF], F32)
        gate_sums = weight_passes((N_TILE,) * FF_TILES, x_codes, x_scales, gate_groups, gate_planes)
        for j in range(FF_TILES):
            nc.scalar.activation(
                out=gate_act[:, N_TILE * j : N_TILE * (j + 1)], in_=gate_sums[j][:],
                func=mybir.ActivationFunctionType.Silu,
            )
        h_rows = keep.tile([P, D_FF], BF16)
        h_codes = keep.tile([P, FF_GROUPS * P], U32, align_bytes=64)
        h_scales = keep.tile([P, FF_GROUPS * P], U8, align_bytes=64)
        up_sums = weight_passes((N_TILE,) * FF_TILES, x_codes, x_scales, up_groups, up_planes)
        for j in range(FF_TILES):
            cols = slice(N_TILE * j, N_TILE * (j + 1))
            nc.vector.tensor_tensor(
                out=h_rows[:, cols], in0=gate_act[:, cols], in1=up_sums[j][:],
                op=mybir.AluOpType.mult,
            )
        for c in range(D_FF // FLIP_COLS):
            token_cols = slice(FLIP_GROUPS * P * c, FLIP_GROUPS * P * (c + 1))
            quantise_tokens(
                nc, banks, stage, identity[:], h_rows[:, FLIP_COLS * c : FLIP_COLS * (c + 1)],
                h_codes[:, token_cols], h_scales[:, token_cols],
            )

        y_sums = weight_passes(Y_WIDTHS, h_codes, h_scales, down_groups, down_planes)
        for j in range(MODEL_TILES):
            y = results.tile([P, N_TILE], F32, align_bytes=DMA_ALIGN)
            if j < MODEL_TILES - 1:
                if j % 2 == 0:
                    nc.vector.tensor_copy(out=y[:], in_=y_sums[j][:])
                else:
                    nc.scalar.copy(out=y[:], in_=y_sums[j][:])
            else:
                nc.vector.tensor_copy(out=y[:, : N_TILE // 2], in_=y_sums[j][:])
                nc.scalar.copy(out=y[:, N_TILE // 2 :], in_=y_sums[j + 1][:])
            nc.sync.dma_start(out=out_rows[:, N_TILE * j : N_TILE * (j + 1)], in_=y[:])
